import numpy as np
import ml_dtypes


def mxq(x, axis, fmt="e4m3"):
    dtype, down = {"e4m3": (ml_dtypes.float8_e4m3fn, 7), "e5m2": (ml_dtypes.float8_e5m2, 14)}[fmt]
    v = np.moveaxis(np.asarray(x, np.float32).astype(ml_dtypes.bfloat16).astype(np.float64), axis, -1)
    blocks = v.reshape(v.shape[:-1] + (-1, 32))
    amax = np.abs(blocks).max(-1, keepdims=True)
    byte = np.maximum(np.where(amax > 0, np.frexp(amax)[1] - 1 + 127, 0) - down, 1)
    scale = np.exp2(byte - 127.0)
    codes = (blocks / scale).astype(np.float32).astype(dtype).astype(np.float64)
    return np.moveaxis((codes * scale).reshape(v.shape), -1, axis)


WIDE = False


def mx_kscale(k):
    if not WIDE:
        return np.ones(k)
    levels = np.array([10, -10, 5, -5, 0])
    a = np.random.permutation(np.resize(levels, k // 512 * 4)).reshape(k // 512, 4)
    idx = np.arange(k)
    return np.exp2(a[idx // 512, idx % 128 // 32])


BF16 = ml_dtypes.bfloat16


def bf(x):
    return np.asarray(x, np.float32).astype(BF16)


def f64(x):
    return np.asarray(x).astype(np.float64)


E2M1 = np.array([0.0, 0.5, 1.0, 1.5, 2.0, 3.0, 4.0, 6.0, -0.0, -0.5, -1.0, -1.5, -2.0, -3.0, -4.0, -6.0])


def pack_weight(w, fmt):
    k, n = w.shape
    w = f64(bf(w)).reshape(k // 32, 32, n)
    amax = np.abs(w).max(1)
    if fmt == "e4m3":
        byte = np.frexp(amax)[1] - 1 + 127 - 7
    else:
        mant, ex = np.frexp(amax / 6.0)
        byte = np.where(mant > 0.5, ex, ex - 1) + 127
    byte = np.clip(np.where(amax > 0, byte, 1), 1, 254)
    scaled = (w * np.exp2(127.0 - byte)[:, None, :]).reshape(k, n).astype(np.float32)
    by_word = np.ascontiguousarray(scaled.reshape(k // 512, 128, 4, n).transpose(0, 1, 3, 2))
    if fmt == "e4m3":
        words = by_word.astype(ml_dtypes.float8_e4m3fn).view(np.uint8)
    else:
        c = by_word.astype(ml_dtypes.float4_e2m1fn).view(np.uint8) & 0xF
        words = c[..., 0::2] | (c[..., 1::2] << 4)
    return np.ascontiguousarray(words), np.ascontiguousarray(byte.astype(np.uint8).reshape(k // 512, 16, n))


def unpack_weight(words, scales, fmt):
    g, p, n, _ = words.shape
    if fmt == "e4m3":
        vals = np.ascontiguousarray(words).view(ml_dtypes.float8_e4m3fn).astype(np.float64)
    else:
        nib = np.empty((g, p, n, 4), np.uint8)
        nib[..., 0::2] = words & 0xF
        nib[..., 1::2] = words >> 4
        vals = E2M1[nib]
    vals = vals * np.repeat(np.exp2(scales.astype(np.float64) - 127.0), 8, axis=1)[..., None]
    return vals.transpose(0, 1, 3, 2).reshape(g * 512, n)


N, M, C, C0, C1 = 128, 2, 128, 8192, 1024
EPS = 1e-3


def bn_relu(y, gamma, beta):
    mean = y.mean(axis=(0, 1))
    var = y.var(axis=(0, 1))
    return np.maximum((y - mean) * (1.0 / np.sqrt(var + EPS)) * gamma + beta, 0.0)


def setup_inputs():
    t = mx_kscale(C0)
    r0 = 0.05 * 4.0 ** np.random.random(C0)
    voxel_feats = bf(np.random.standard_normal((N, M, C)) + 0.5 * np.random.standard_normal(C))
    W0 = bf(np.random.standard_normal((C0, C)) / np.sqrt(C) * r0[:, None])
    gamma0 = bf((1.0 + 0.1 * np.random.standard_normal(C0)) * t)
    beta0 = bf(0.2 * np.random.standard_normal(C0) * t)
    W1 = np.random.standard_normal((C1, 2 * C0)) * 0.2 / np.sqrt(2 * C0) / np.concatenate([t, t])[None, :]
    W1_words, W1_scales = pack_weight(np.ascontiguousarray(W1.T), "e4m3")
    gamma1 = bf(1.0 + 0.1 * np.random.standard_normal(C1))
    beta1 = bf(0.3 * np.random.standard_normal(C1) - 0.5)
    return {"voxel_feats": voxel_feats,
            "W0": W0,
            "gamma0": gamma0,
            "beta0": beta0,
            "W1_words": W1_words,
            "W1_scales": W1_scales,
            "gamma1": gamma1,
            "beta1": beta1}


def reference(voxel_feats, W0, gamma0, beta0, W1_words, W1_scales, gamma1, beta1):
    y0 = f64(voxel_feats) @ f64(W0).T
    p = bn_relu(y0, f64(gamma0), f64(beta0))
    a = p.max(axis=1, keepdims=True)
    x1 = np.concatenate([mxq(p, 2, "e4m3"), np.broadcast_to(mxq(a, 2, "e4m3"), (N, M, C0))], axis=2)
    y1 = x1 @ unpack_weight(W1_words, W1_scales, "e4m3")
    return bn_relu(y1, f64(gamma1), f64(beta1)).max(axis=1)

@@ -1,0 +1,338 @@
+from contextlib import ExitStack
+
+import concourse.mybir as mybir
+from concourse.masks import make_identity
+
+F32 = mybir.dt.float32
+BF16 = mybir.dt.bfloat16
+I32 = mybir.dt.int32
+U32 = mybir.dt.uint32
+U8 = mybir.dt.uint8
+FP8X4 = mybir.dt.float8_e4m3fn_x4
+ACT = mybir.ActivationFunctionType
+ALU = mybir.AluOpType
+
+P = 128
+PACK = 4
+K_PASS = P * PACK
+VOXELS = 128
+POINTS = 2
+ROWS = VOXELS * POINTS
+C_IN = 128
+C0 = 8192
+C1 = 1024
+GROUPS = C0 // K_PASS
+N_HALF = 512
+HALVES = C1 // N_HALF
+CHUNKS = C1 // P
+EPS = 1e-3
+PLANES = 4
+
+FLOPS = 2 * ROWS * C_IN * C0 + 2 * ROWS * 2 * C0 * C1
+
+
+def tile_vfe_k_kernel(tc, voxel_feats, W0, gamma0, beta0, W1_words, W1_scales, gamma1, beta1, out):
+    nc = tc.nc
+    with ExitStack() as ctx:
+        keep = ctx.enter_context(tc.tile_pool(name="keep", bufs=1))
+        ring = ctx.enter_context(tc.tile_pool(name="ring", bufs=3))
+        acc_pool = ctx.enter_context(tc.psum_pool(name="acc", bufs=1))
+        work = ctx.enter_context(tc.psum_pool(name="work", bufs=4))
+
+        vf_sb = keep.tile([P, POINTS, C_IN], BF16, name="vf_sb")
+        nc.sync.dma_start(out=vf_sb[:], in_=voxel_feats)
+
+        params = keep.tile([P, K_PASS + P], BF16, name="params")
+        nc.vector.memset(params[:], 0.0)
+        w_planes = keep.tile([P, 2 * GROUPS // PLANES, C1], U8, name="w_planes", align_bytes=64)
+        nc.vector.memset(w_planes[:].bitcast(I32), 0)
+
+        ident_bf = keep.tile([P, P], BF16, name="ident_bf")
+        make_identity(nc, ident_bf[:])
+        ident_f32 = keep.tile([P, P], F32, name="ident_f32")
+        make_identity(nc, ident_f32[:])
+
+        w0T = [keep.tile([P, 2 * PACK, P], BF16, name="w0T%d" % pair) for pair in range(GROUPS // 2)]
+        w_words = [keep.tile([P, C1 * PACK], U8, name="w_words%d" % G, align_bytes=64) for G in range(2 * GROUPS)]
+        vfT = keep.tile([P, ROWS], BF16, name="vfT")
+        gb0 = keep.tile([P, 2, GROUPS, PACK], F32, name="gb0")
+        gb1 = keep.tile([P, 2, CHUNKS], F32, name="gb1")
+
+        with tc.tile_pool(name="w0_rows", bufs=1) as w0_rows:
+            w0_view = W0.rearrange("(g p t) c -> p g (t c)", p=P, t=PACK)
+            w0_sb = [w0_rows.tile([P, 2, PACK * C_IN], BF16, name="w0_sb%d" % pair) for pair in range(GROUPS // 2)]
+            for pair in range(GROUPS // 2):
+                nc.sync.dma_start(out=w0_sb[pair][:], in_=w0_view[:, 2 * pair : 2 * pair + 2, :])
+                if pair == 0:
+                    nc.sync.dma_start(out=params[0:GROUPS, 0:K_PASS], in_=gamma0.rearrange("(g k) -> g k", k=K_PASS))
+                    nc.sync.dma_start(out=params[GROUPS : 2 * GROUPS, 0:K_PASS], in_=beta0.rearrange("(g k) -> g k", k=K_PASS))
+                    nc.sync.dma_start(out=params[0:CHUNKS, K_PASS:], in_=gamma1.rearrange("(j i) -> j i", i=P))
+                    nc.sync.dma_start(out=params[CHUNKS : 2 * CHUNKS, K_PASS:], in_=beta1.rearrange("(j i) -> j i", i=P))
+
+            for i in range(2 * GROUPS // PLANES):
+                for Q in range(4):
+                    nc.sync.dma_start(
+                        out=w_planes[32 * Q : 32 * Q + 16, i, :].bitcast(I32),
+                        in_=W1_scales[PLANES * i : PLANES * (i + 1), 4 * Q : 4 * Q + 4, :].bitcast(I32),
+                    )
+            for g in range(GROUPS):
+                for G in (g, GROUPS + g):
+                    nc.sync.dma_start(
+                        out=w_words[G][:].bitcast(I32),
+                        in_=W1_words[G].rearrange("p n t -> p (n t)").bitcast(I32),
+                    )
+
+            vT_ps = work.tile([P, POINTS, VOXELS], BF16, name="vT_ps", tag="work")
+            for m in range(POINTS):
+                nc.tensor.transpose(vT_ps[:, m, :], vf_sb[:, m, :], ident_bf[:])
+            nc.vector.tensor_copy(out=vfT[:], in_=vT_ps[:].rearrange("c m v -> c (m v)"))
+
+            for pair in range(GROUPS // 2):
+                wT_ps = work.tile([P, 2 * PACK, P], BF16, name="wT_ps", tag="work")
+                for j in range(2 * PACK):
+                    nc.tensor.transpose(wT_ps[:, j, :], w0_sb[pair][:, j // PACK, (j % PACK) * C_IN : (j % PACK + 1) * C_IN], ident_bf[:])
+                if pair % 2 == 0:
+                    nc.vector.tensor_copy(out=w0T[pair][:], in_=wT_ps[:])
+                else:
+                    nc.scalar.copy(out=w0T[pair][:], in_=wT_ps[:])
+                if pair == 0:
+                    pT_ps = work.tile([P, PACK + 1, P], BF16, name="pT_ps", tag="work")
+                    for t in range(PACK):
+                        nc.tensor.transpose(pT_ps[:, t, :], params[:, t:K_PASS:PACK], ident_bf[:])
+                    nc.tensor.transpose(pT_ps[:, PACK, :], params[:, K_PASS:], ident_bf[:])
+                    nc.vector.tensor_copy(
+                        out=gb0[:], in_=pT_ps[:, 0:PACK, 0 : 2 * GROUPS].rearrange("p t (w g) -> p w g t", w=2)
+                    )
+                    nc.vector.tensor_copy(
+                        out=gb1[:], in_=pT_ps[:, PACK, 0 : 2 * CHUNKS].rearrange("p (w j) -> p w j", w=2)
+                    )
+
+        tail = ctx.enter_context(tc.tile_pool(name="tail", bufs=2))
+
+        def weight_operands(G, h):
+            k = PLANES * (G % PLANES)
+            words = w_words[G][:, h * N_HALF * PACK : (h + 1) * N_HALF * PACK].bitcast(FP8X4)
+            return words, w_planes[k:P, G // PLANES, h * N_HALF : (h + 1) * N_HALF]
+
+        acc = [[acc_pool.tile([P, N_HALF], F32, name="acc%d%d" % (m, h)) for h in range(HALVES)] for m in range(POINTS)]
+
+        mean_var = {}
+        bn = {}
+
+        def bn_tile(key, name, width):
+            bn[key, name] = ring.tile([P, width], F32, name=name + str(width))
+            return bn[key, name]
+
+        def bn_root(key, width):
+            nc.scalar.activation(out=bn_tile(key, "std", width)[:], in_=mean_var[key][:, :, 1], func=ACT.Sqrt, bias=EPS, scale=1.0)
+
+        def bn_mean_gamma(key, width, gamma):
+            nc.vector.tensor_tensor(out=bn_tile(key, "mg", width)[:], in0=mean_var[key][:, :, 0], in1=gamma, op=ALU.mult)
+
+        def bn_reciprocal(key, width):
+            nc.vector.reciprocal(out=bn_tile(key, "rstd", width)[:], in_=bn[key, "std"][:])
+
+        def bn_mean_scale(key, width):
+            nc.vector.tensor_tensor(out=bn_tile(key, "ms", width)[:], in0=bn[key, "mg"][:], in1=bn[key, "rstd"][:], op=ALU.mult)
+
+        def bn_scale(key, width, gamma):
+            nc.vector.tensor_tensor(out=bn_tile(key, "s", width)[:], in0=gamma, in1=bn[key, "rstd"][:], op=ALU.mult)
+
+        def bn_bias(key, width, beta):
+            nc.vector.tensor_tensor(out=bn_tile(key, "b", width)[:], in0=beta, in1=bn[key, "ms"][:], op=ALU.subtract)
+
+        y0 = {}
+        stats = {}
+        planes = {}
+        grouped = {}
+        a_grouped = {}
+        x_codes = {}
+        x_scales = {}
+
+        def is_group(g):
+            return 0 <= g < GROUPS
+
+        def layer0_matmuls(g):
+            for u in range(2):
+                y0[g, u] = work.tile([P, 2, ROWS], F32, name="y0_ps", tag="work")
+                for e in range(2):
+                    nc.tensor.matmul(y0[g, u][:, e, :], lhsT=w0T[g // 2][:, (g % 2) * PACK + 2 * u + e, :], rhs=vfT[:], start=True, stop=True)
+            stats[g] = ring.tile([P, PACK, 6], F32, name="stats")
+            mean_var[g] = ring.tile([P, PACK, 2], F32, name="mean_var")
+
+        def statistics(g, t):
+            nc.vector.bn_stats(out=stats[g][:, t, :], in_=y0[g, t // 2][:, t % 2, :])
+
+        def aggregate(g, t):
+            nc.vector.bn_aggr(out=mean_var[g][:, t, :], in_=stats[g][:, t, :])
+
+        def normalise_relu(g):
+            planes[g] = ring.tile([P, PACK, ROWS], BF16, name="planes")
+            for t in range(PACK):
+                nc.scalar.activation(out=planes[g][:, t, :], in_=y0[g, t // 2][:, t % 2, :], func=ACT.Relu, bias=bn[g, "b"][:, t : t + 1], scale=bn[g, "s"][:, t : t + 1])
+
+        def regroup(g):
+            grouped[g] = ring.tile([P, POINTS, VOXELS, PACK], BF16, name="grouped", align_bytes=64)
+            for m in range(POINTS):
+                nc.scalar.copy(
+                    out=grouped[g][:, m].rearrange("p (c i) t -> p c t i", i=4),
+                    in_=planes[g][:, :, m * VOXELS : (m + 1) * VOXELS].rearrange("p t (c i) -> p c t i", i=4),
+                )
+
+        def maximum(g):
+            a_grouped[g] = ring.tile([P, VOXELS, PACK], BF16, name="a_grouped", align_bytes=64)
+            nc.vector.tensor_tensor(out=a_grouped[g][:], in0=grouped[g][:, 0], in1=grouped[g][:, 1], op=ALU.max)
+
+        def quantise_p(g):
+            x_codes[g] = ring.tile([P, POINTS + 1, VOXELS], U32, name="x_codes", align_bytes=64)
+            x_scales[g] = ring.tile([P, POINTS + 1, VOXELS], U8, name="x_scales", align_bytes=64)
+            nc.vector.quantize_mx(
+                out=x_codes[g][:, 0:POINTS, :].rearrange("p m v -> p (m v)").bitcast(FP8X4),
+                scales=x_scales[g][:, 0:POINTS, :].rearrange("p m v -> p (m v)"),
+                in_=grouped[g][:].rearrange("p m v t -> p (m v t)"),
+            )
+
+        def quantise_a(g):
+            nc.vector.quantize_mx(out=x_codes[g][:, POINTS, :].bitcast(FP8X4), scales=x_scales[g][:, POINTS, :], in_=a_grouped[g][:].rearrange("p v t -> p (v t)"))
+
+        def mx_passes(g):
+            for h in range(HALVES):
+                for m in range(POINTS):
+                    for operand, G in ((m, g), (POINTS, GROUPS + g)):
+                        words, plane = weight_operands(G, h)
+                        nc.tensor.matmul_mx(
+                            acc[m][h][:],
+                            lhsT=x_codes[g][:, operand, :].bitcast(FP8X4),
+                            lhsT_scale=x_scales[g][:, operand, :],
+                            rhs=words,
+                            rhs_scale=plane,
+                            start=(G == 0),
+                            stop=(G == 2 * GROUPS - 1),
+                        )
+
+        with tc.manual_schedule():
+            for i in range(-2, GROUPS + 1):
+                done, soon, new = i - 1, i + 1, i + 2
+                if is_group(i):
+                    normalise_relu(i)
+                if is_group(soon):
+                    bn_root(soon, PACK)
+                if is_group(i):
+                    regroup(i)
+                if is_group(new):
+                    layer0_matmuls(new)
+                if is_group(done):
+                    maximum(done)
+                if is_group(soon):
+                    bn_mean_gamma(soon, PACK, gb0[:, 0, soon, :])
+                if is_group(done):
+                    quantise_p(done)
+                    quantise_a(done)
+                    mx_passes(done)
+                if is_group(soon):
+                    bn_reciprocal(soon, PACK)
+                if is_group(new):
+                    statistics(new, 0)
+                if is_group(soon):
+                    bn_mean_scale(soon, PACK)
+                    bn_scale(soon, PACK, gb0[:, 0, soon, :])
+                if is_group(new):
+                    statistics(new, 1)
+                if is_group(soon):
+                    bn_bias(soon, PACK, gb0[:, 1, soon, :])
+                if is_group(new):
+                    statistics(new, 2)
+                    aggregate(new, 0)
+                    statistics(new, 3)
+                    aggregate(new, 1)
+                    aggregate(new, 2)
+                    aggregate(new, 3)
+
+            y_sb = {}
+            yT = {}
+            stats1 = {}
+            z = {}
+            z_max = {}
+            o_ps = {}
+
+            def leave_psum(h):
+                y_sb[h] = tail.tile([P, POINTS, N_HALF], F32, name="y_sb")
+                nc.scalar.copy(out=y_sb[h][:, 0, :], in_=acc[0][h][:])
+                nc.vector.tensor_copy(out=y_sb[h][:, 1, :], in_=acc[1][h][:])
+
+            def channels_to_partitions(h):
+                for pair in range(2):
+                    yT[h, pair] = work.tile([P, 2, ROWS], F32, name="yT_ps", tag="work")
+                    for c in range(2):
+                        for m in range(POINTS):
+                            nc.tensor.transpose(yT[h, pair][:, c, m * VOXELS : (m + 1) * VOXELS], y_sb[h][:, m, (2 * pair + c) * P : (2 * pair + c + 1) * P], ident_f32[:])
+                stats1[h] = tail.tile([P, 4, 6], F32, name="stats1")
+                mean_var["y1", h] = tail.tile([P, 4, 2], F32, name="mean_var1")
+
+            def statistics1(h, c):
+                nc.vector.bn_stats(out=stats1[h][:, c, :], in_=yT[h, c // 2][:, c % 2, :])
+
+            def aggregate1(h, c):
+                nc.vector.bn_aggr(out=mean_var["y1", h][:, c, :], in_=stats1[h][:, c, :])
+
+            def normalise_relu1(h):
+                z[h] = tail.tile([P, 4, POINTS, VOXELS], F32, name="z")
+                for c in range(4):
+                    nc.scalar.activation(out=z[h][:, c].rearrange("p m v -> p (m v)"), in_=yT[h, c // 2][:, c % 2, :], func=ACT.Relu, bias=bn[("y1", h), "b"][:, c : c + 1], scale=bn[("y1", h), "s"][:, c : c + 1])
+                z_max[h] = tail.tile([P, 4, VOXELS], F32, name="z_max")
+                o_ps[h] = work.tile([P, 4, P], F32, name="o_ps", tag="work")
+
+            def maximum_over_points(h, pair):
+                chunks = slice(2 * pair, 2 * pair + 2)
+                nc.vector.tensor_tensor(out=z_max[h][:, chunks, :], in0=z[h][:, chunks, 0, :], in1=z[h][:, chunks, 1, :], op=ALU.max)
+                for c in range(2 * pair, 2 * pair + 2):
+                    nc.tensor.transpose(o_ps[h][:, c, :], z_max[h][:, c, :], ident_f32[:])
+
+            def store(h, copy):
+                o_sb = tail.tile([P, N_HALF], F32, name="o_sb")
+                copy(out=o_sb[:], in_=o_ps[h][:].rearrange("v c n -> v (c n)"))
+                nc.sync.dma_start(out=out[:, h * N_HALF : (h + 1) * N_HALF], in_=o_sb[:])
+
+            gamma1_sb = [gb1[:, 0, 4 * h : 4 * h + 4] for h in range(HALVES)]
+            beta1_sb = [gb1[:, 1, 4 * h : 4 * h + 4] for h in range(HALVES)]
+            first, second = ("y1", 0), ("y1", 1)
+            leave_psum(0)
+            leave_psum(1)
+            channels_to_partitions(0)
+            channels_to_partitions(1)
+            statistics1(0, 0)
+            statistics1(0, 1)
+            statistics1(0, 2)
+            aggregate1(0, 0)
+            statistics1(0, 3)
+            aggregate1(0, 1)
+            aggregate1(0, 2)
+            statistics1(1, 0)
+            aggregate1(0, 3)
+            bn_root(first, 4)
+            statistics1(1, 1)
+            bn_mean_gamma(first, 4, gamma1_sb[0])
+            statistics1(1, 2)
+            bn_reciprocal(first, 4)
+            statistics1(1, 3)
+            bn_mean_scale(first, 4)
+            bn_scale(first, 4, gamma1_sb[0])
+            aggregate1(1, 0)
+            aggregate1(1, 1)
+            bn_bias(first, 4, beta1_sb[0])
+            aggregate1(1, 2)
+            aggregate1(1, 3)
+            bn_root(second, 4)
+            normalise_relu1(0)
+            bn_mean_gamma(second, 4, gamma1_sb[1])
+            bn_reciprocal(second, 4)
+            bn_mean_scale(second, 4)
+            bn_scale(second, 4, gamma1_sb[1])
+            bn_bias(second, 4, beta1_sb[1])
+            normalise_relu1(1)
+            maximum_over_points(0, 0)
+            maximum_over_points(0, 1)
+            maximum_over_points(1, 0)
+            maximum_over_points(1, 1)
+            store(0, nc.vector.tensor_copy)
+            store(1, nc.scalar.copy)

@@ -34,87 +34,34 @@ FLOPS = 2 * ROWS * C_IN * C0 + 2 * ROWS * 2 * C0 * C1
 def tile_vfe_k_kernel(tc, voxel_feats, W0, gamma0, beta0, W1_words, W1_scales, gamma1, beta1, out):
     nc = tc.nc
     with ExitStack() as ctx:
+        ctx.enter_context(tc.manual_schedule())
         keep = ctx.enter_context(tc.tile_pool(name="keep", bufs=1))
         ring = ctx.enter_context(tc.tile_pool(name="ring", bufs=3))
-        acc_pool = ctx.enter_context(tc.psum_pool(name="acc", bufs=1))
         work = ctx.enter_context(tc.psum_pool(name="work", bufs=4))
 
         vf_sb = keep.tile([P, POINTS, C_IN], BF16, name="vf_sb")
-        nc.sync.dma_start(out=vf_sb[:], in_=voxel_feats)
-
-        params = keep.tile([P, K_PASS + P], BF16, name="params")
-        nc.vector.memset(params[:], 0.0)
-        w_planes = keep.tile([P, 2 * GROUPS // PLANES, C1], U8, name="w_planes", align_bytes=64)
-        nc.vector.memset(w_planes[:].bitcast(I32), 0)
-
-        ident_bf = keep.tile([P, P], BF16, name="ident_bf")
-        make_identity(nc, ident_bf[:])
-        ident_f32 = keep.tile([P, P], F32, name="ident_f32")
-        make_identity(nc, ident_f32[:])
-
-        w0T = [keep.tile([P, 2 * PACK, P], BF16, name="w0T%d" % pair) for pair in range(GROUPS // 2)]
-        w_words = [keep.tile([P, C1 * PACK], U8, name="w_words%d" % G, align_bytes=64) for G in range(2 * GROUPS)]
         vfT = keep.tile([P, ROWS], BF16, name="vfT")
+        params = keep.tile([P, K_PASS + P], BF16, name="params")
         gb0 = keep.tile([P, 2, GROUPS, PACK], F32, name="gb0")
         gb1 = keep.tile([P, 2, CHUNKS], F32, name="gb1")
+        w0T = [keep.tile([P, 2 * PACK, P], BF16, name="w0T%d" % pair) for pair in range(GROUPS // 2)]
+        w_words = [keep.tile([P, C1 * PACK], U8, name="w_words%d" % G, align_bytes=64) for G in range(2 * GROUPS)]
+        w_planes = keep.tile([P, 2 * GROUPS // PLANES, C1], U8, name="w_planes", align_bytes=64)
+        ident_bf = keep.tile([P, P], BF16, name="ident_bf")
+        ident_f32 = keep.tile([P, P], F32, name="ident_f32")
+        warm = keep.tile([P, 2], F32, name="warm")
 
-        with tc.tile_pool(name="w0_rows", bufs=1) as w0_rows:
-            w0_view = W0.rearrange("(g p t) c -> p g (t c)", p=P, t=PACK)
-            w0_sb = [w0_rows.tile([P, 2, PACK * C_IN], BF16, name="w0_sb%d" % pair) for pair in range(GROUPS // 2)]
-            for pair in range(GROUPS // 2):
-                nc.sync.dma_start(out=w0_sb[pair][:], in_=w0_view[:, 2 * pair : 2 * pair + 2, :])
-                if pair == 0:
-                    nc.sync.dma_start(out=params[0:GROUPS, 0:K_PASS], in_=gamma0.rearrange("(g k) -> g k", k=K_PASS))
-                    nc.sync.dma_start(out=params[GROUPS : 2 * GROUPS, 0:K_PASS], in_=beta0.rearrange("(g k) -> g k", k=K_PASS))
-                    nc.sync.dma_start(out=params[0:CHUNKS, K_PASS:], in_=gamma1.rearrange("(j i) -> j i", i=P))
-                    nc.sync.dma_start(out=params[CHUNKS : 2 * CHUNKS, K_PASS:], in_=beta1.rearrange("(j i) -> j i", i=P))
-
-            for i in range(2 * GROUPS // PLANES):
-                for Q in range(4):
-                    nc.sync.dma_start(
-                        out=w_planes[32 * Q : 32 * Q + 16, i, :].bitcast(I32),
-                        in_=W1_scales[PLANES * i : PLANES * (i + 1), 4 * Q : 4 * Q + 4, :].bitcast(I32),
-                    )
-            for g in range(GROUPS):
-                for G in (g, GROUPS + g):
-                    nc.sync.dma_start(
-                        out=w_words[G][:].bitcast(I32),
-                        in_=W1_words[G].rearrange("p n t -> p (n t)").bitcast(I32),
-                    )
-
-            vT_ps = work.tile([P, POINTS, VOXELS], BF16, name="vT_ps", tag="work")
-            for m in range(POINTS):
-                nc.tensor.transpose(vT_ps[:, m, :], vf_sb[:, m, :], ident_bf[:])
-            nc.vector.tensor_copy(out=vfT[:], in_=vT_ps[:].rearrange("c m v -> c (m v)"))
-
-            for pair in range(GROUPS // 2):
-                wT_ps = work.tile([P, 2 * PACK, P], BF16, name="wT_ps", tag="work")
-                for j in range(2 * PACK):
-                    nc.tensor.transpose(wT_ps[:, j, :], w0_sb[pair][:, j // PACK, (j % PACK) * C_IN : (j % PACK + 1) * C_IN], ident_bf[:])
-                if pair % 2 == 0:
-                    nc.vector.tensor_copy(out=w0T[pair][:], in_=wT_ps[:])
-                else:
-                    nc.scalar.copy(out=w0T[pair][:], in_=wT_ps[:])
-                if pair == 0:
-                    pT_ps = work.tile([P, PACK + 1, P], BF16, name="pT_ps", tag="work")
-                    for t in range(PACK):
-                        nc.tensor.transpose(pT_ps[:, t, :], params[:, t:K_PASS:PACK], ident_bf[:])
-                    nc.tensor.transpose(pT_ps[:, PACK, :], params[:, K_PASS:], ident_bf[:])
-                    nc.vector.tensor_copy(
-                        out=gb0[:], in_=pT_ps[:, 0:PACK, 0 : 2 * GROUPS].rearrange("p t (w g) -> p w g t", w=2)
-                    )
-                    nc.vector.tensor_copy(
-                        out=gb1[:], in_=pT_ps[:, PACK, 0 : 2 * CHUNKS].rearrange("p (w j) -> p w j", w=2)
-                    )
-
-        tail = ctx.enter_context(tc.tile_pool(name="tail", bufs=2))
+        nc.vector.memset(warm[:], 1.0)
+        nc.scalar.activation(out=warm[:, 1:2], in_=warm[:, 0:1], func=ACT.Sqrt)
+        nc.vector.memset(params[:], 0.0)
+        nc.vector.memset(w_planes[:].bitcast(I32), 0)
+        make_identity(nc, ident_bf[:])
+        make_identity(nc, ident_f32[:])
 
         def weight_operands(G, h):
             k = PLANES * (G % PLANES)
             words = w_words[G][:, h * N_HALF * PACK : (h + 1) * N_HALF * PACK].bitcast(FP8X4)
             return words, w_planes[k:P, G // PLANES, h * N_HALF : (h + 1) * N_HALF]
-
-        acc = [[acc_pool.tile([P, N_HALF], F32, name="acc%d%d" % (m, h)) for h in range(HALVES)] for m in range(POINTS)]
 
         mean_var = {}
         bn = {}
@@ -210,129 +157,185 @@ def tile_vfe_k_kernel(tc, voxel_feats, W0, gamma0, beta0, W1_words, W1_scales, g
                             stop=(G == 2 * GROUPS - 1),
                         )
 
-        with tc.manual_schedule():
-            for i in range(-2, GROUPS + 1):
-                done, soon, new = i - 1, i + 1, i + 2
-                if is_group(i):
-                    normalise_relu(i)
-                if is_group(soon):
-                    bn_root(soon, PACK)
-                if is_group(i):
-                    regroup(i)
-                if is_group(new):
-                    layer0_matmuls(new)
-                if is_group(done):
-                    maximum(done)
-                if is_group(soon):
-                    bn_mean_gamma(soon, PACK, gb0[:, 0, soon, :])
-                if is_group(done):
-                    quantise_p(done)
-                    quantise_a(done)
-                    mx_passes(done)
-                if is_group(soon):
-                    bn_reciprocal(soon, PACK)
-                if is_group(new):
-                    statistics(new, 0)
-                if is_group(soon):
-                    bn_mean_scale(soon, PACK)
-                    bn_scale(soon, PACK, gb0[:, 0, soon, :])
-                if is_group(new):
-                    statistics(new, 1)
-                if is_group(soon):
-                    bn_bias(soon, PACK, gb0[:, 1, soon, :])
-                if is_group(new):
-                    statistics(new, 2)
-                    aggregate(new, 0)
-                    statistics(new, 3)
-                    aggregate(new, 1)
-                    aggregate(new, 2)
-                    aggregate(new, 3)
+        def step(i):
+            done, soon, new = i - 1, i + 1, i + 2
+            if is_group(i):
+                normalise_relu(i)
+            if is_group(soon):
+                bn_root(soon, PACK)
+            if is_group(i):
+                regroup(i)
+            if is_group(new):
+                layer0_matmuls(new)
+            if is_group(done):
+                maximum(done)
+            if is_group(soon):
+                bn_mean_gamma(soon, PACK, gb0[:, 0, soon, :])
+            if is_group(done):
+                quantise_p(done)
+                quantise_a(done)
+                mx_passes(done)
+            if is_group(soon):
+                bn_reciprocal(soon, PACK)
+            if is_group(new):
+                statistics(new, 0)
+            if is_group(soon):
+                bn_mean_scale(soon, PACK)
+                bn_scale(soon, PACK, gb0[:, 0, soon, :])
+            if is_group(new):
+                statistics(new, 1)
+            if is_group(soon):
+                bn_bias(soon, PACK, gb0[:, 1, soon, :])
+            if is_group(new):
+                statistics(new, 2)
+                aggregate(new, 0)
+                statistics(new, 3)
+                aggregate(new, 1)
+                aggregate(new, 2)
+                aggregate(new, 3)
 
-            y_sb = {}
-            yT = {}
-            stats1 = {}
-            z = {}
-            z_max = {}
-            o_ps = {}
+        with tc.tile_pool(name="w0_rows", bufs=1) as w0_rows, tc.psum_pool(name="turn", bufs=4) as turn:
+            nc.sync.dma_start(out=vf_sb[:], in_=voxel_feats)
+            w0_view = W0.rearrange("(g p t) c -> p g (t c)", p=P, t=PACK)
+            w0_sb = [w0_rows.tile([P, 2 * PACK, C_IN], BF16, name="w0_sb%d" % pair) for pair in range(GROUPS // 2)]
+            for pair in range(GROUPS // 2):
+                nc.sync.dma_start(out=w0_sb[pair][:].rearrange("p (g t) c -> p g (t c)", g=2), in_=w0_view[:, 2 * pair : 2 * pair + 2, :])
+                if pair == 0:
+                    nc.sync.dma_start(out=params[0:GROUPS, 0:K_PASS], in_=gamma0.rearrange("(g k) -> g k", k=K_PASS))
+                    nc.sync.dma_start(out=params[GROUPS : 2 * GROUPS, 0:K_PASS], in_=beta0.rearrange("(g k) -> g k", k=K_PASS))
+                    nc.sync.dma_start(out=params[0:CHUNKS, K_PASS:], in_=gamma1.rearrange("(j i) -> j i", i=P))
+                    nc.sync.dma_start(out=params[CHUNKS : 2 * CHUNKS, K_PASS:], in_=beta1.rearrange("(j i) -> j i", i=P))
+            for batch in range(GROUPS // PLANES):
+                for i in (batch, GROUPS // PLANES + batch):
+                    for Q in range(4):
+                        nc.sync.dma_start(
+                            out=w_planes[32 * Q : 32 * Q + 16, i, :].bitcast(I32),
+                            in_=W1_scales[PLANES * i : PLANES * (i + 1), 4 * Q : 4 * Q + 4, :].bitcast(I32),
+                        )
+                for g in range(PLANES * batch, PLANES * (batch + 1)):
+                    for G in (g, GROUPS + g):
+                        nc.sync.dma_start(out=w_words[G][:].bitcast(I32), in_=W1_words[G].rearrange("p n t -> p (n t)").bitcast(I32))
 
-            def leave_psum(h):
-                y_sb[h] = tail.tile([P, POINTS, N_HALF], F32, name="y_sb")
-                nc.scalar.copy(out=y_sb[h][:, 0, :], in_=acc[0][h][:])
-                nc.vector.tensor_copy(out=y_sb[h][:, 1, :], in_=acc[1][h][:])
+            def turn_w0(pair):
+                wT_ps = turn.tile([P, 2 * PACK, P], BF16, name="wT_ps")
+                for j in range(2 * PACK):
+                    nc.tensor.transpose(wT_ps[:, j, :], w0_sb[pair][:, j, :], ident_bf[:])
+                if pair % 2 == 0:
+                    nc.vector.tensor_copy(out=w0T[pair][:], in_=wT_ps[:])
+                else:
+                    nc.scalar.copy(out=w0T[pair][:], in_=wT_ps[:])
 
-            def channels_to_partitions(h):
-                for pair in range(2):
-                    yT[h, pair] = work.tile([P, 2, ROWS], F32, name="yT_ps", tag="work")
-                    for c in range(2):
-                        for m in range(POINTS):
-                            nc.tensor.transpose(yT[h, pair][:, c, m * VOXELS : (m + 1) * VOXELS], y_sb[h][:, m, (2 * pair + c) * P : (2 * pair + c + 1) * P], ident_f32[:])
-                stats1[h] = tail.tile([P, 4, 6], F32, name="stats1")
-                mean_var["y1", h] = tail.tile([P, 4, 2], F32, name="mean_var1")
+            vT_ps = turn.tile([P, POINTS, VOXELS], BF16, name="vT_ps", tag="wT_ps")
+            for m in range(POINTS):
+                nc.tensor.transpose(vT_ps[:, m, :], vf_sb[:, m, :], ident_bf[:])
+            nc.vector.tensor_copy(out=vfT[:], in_=vT_ps[:].rearrange("c m v -> c (m v)"))
+            turn_w0(0)
 
-            def statistics1(h, c):
-                nc.vector.bn_stats(out=stats1[h][:, c, :], in_=yT[h, c // 2][:, c % 2, :])
+            step(-2)
+            pT_ps = turn.tile([P, PACK + 1, P], BF16, name="pT_ps", tag="wT_ps")
+            for t in range(PACK):
+                nc.tensor.transpose(pT_ps[:, t, :], params[:, t:K_PASS:PACK], ident_bf[:])
+            nc.tensor.transpose(pT_ps[:, PACK, :], params[:, K_PASS:], ident_bf[:])
+            nc.vector.tensor_copy(out=gb0[:], in_=pT_ps[:, 0:PACK, 0 : 2 * GROUPS].rearrange("p t (w g) -> p w g t", w=2))
+            nc.vector.tensor_copy(out=gb1[:], in_=pT_ps[:, PACK, 0 : 2 * CHUNKS].rearrange("p (w j) -> p w j", w=2))
+            for pair in range(1, GROUPS // 4):
+                turn_w0(pair)
+            step(-1)
+            for pair in range(GROUPS // 4, GROUPS // 2):
+                turn_w0(pair)
 
-            def aggregate1(h, c):
-                nc.vector.bn_aggr(out=mean_var["y1", h][:, c, :], in_=stats1[h][:, c, :])
+        tail = ctx.enter_context(tc.tile_pool(name="tail", bufs=2))
+        acc_pool = ctx.enter_context(tc.psum_pool(name="acc", bufs=1))
+        acc = [[acc_pool.tile([P, N_HALF], F32, name="acc%d%d" % (m, h)) for h in range(HALVES)] for m in range(POINTS)]
 
-            def normalise_relu1(h):
-                z[h] = tail.tile([P, 4, POINTS, VOXELS], F32, name="z")
-                for c in range(4):
-                    nc.scalar.activation(out=z[h][:, c].rearrange("p m v -> p (m v)"), in_=yT[h, c // 2][:, c % 2, :], func=ACT.Relu, bias=bn[("y1", h), "b"][:, c : c + 1], scale=bn[("y1", h), "s"][:, c : c + 1])
-                z_max[h] = tail.tile([P, 4, VOXELS], F32, name="z_max")
-                o_ps[h] = work.tile([P, 4, P], F32, name="o_ps", tag="work")
+        for i in range(GROUPS + 1):
+            step(i)
 
-            def maximum_over_points(h, pair):
-                chunks = slice(2 * pair, 2 * pair + 2)
-                nc.vector.tensor_tensor(out=z_max[h][:, chunks, :], in0=z[h][:, chunks, 0, :], in1=z[h][:, chunks, 1, :], op=ALU.max)
-                for c in range(2 * pair, 2 * pair + 2):
-                    nc.tensor.transpose(o_ps[h][:, c, :], z_max[h][:, c, :], ident_f32[:])
+        y_sb = {}
+        yT = {}
+        stats1 = {}
+        z = {}
+        z_max = {}
+        o_ps = {}
 
-            def store(h, copy):
-                o_sb = tail.tile([P, N_HALF], F32, name="o_sb")
-                copy(out=o_sb[:], in_=o_ps[h][:].rearrange("v c n -> v (c n)"))
-                nc.sync.dma_start(out=out[:, h * N_HALF : (h + 1) * N_HALF], in_=o_sb[:])
+        def leave_psum(h):
+            y_sb[h] = tail.tile([P, POINTS, N_HALF], F32, name="y_sb")
+            nc.scalar.copy(out=y_sb[h][:, 0, :], in_=acc[0][h][:])
+            nc.vector.tensor_copy(out=y_sb[h][:, 1, :], in_=acc[1][h][:])
 
-            gamma1_sb = [gb1[:, 0, 4 * h : 4 * h + 4] for h in range(HALVES)]
-            beta1_sb = [gb1[:, 1, 4 * h : 4 * h + 4] for h in range(HALVES)]
-            first, second = ("y1", 0), ("y1", 1)
-            leave_psum(0)
-            leave_psum(1)
-            channels_to_partitions(0)
-            channels_to_partitions(1)
-            statistics1(0, 0)
-            statistics1(0, 1)
-            statistics1(0, 2)
-            aggregate1(0, 0)
-            statistics1(0, 3)
-            aggregate1(0, 1)
-            aggregate1(0, 2)
-            statistics1(1, 0)
-            aggregate1(0, 3)
-            bn_root(first, 4)
-            statistics1(1, 1)
-            bn_mean_gamma(first, 4, gamma1_sb[0])
-            statistics1(1, 2)
-            bn_reciprocal(first, 4)
-            statistics1(1, 3)
-            bn_mean_scale(first, 4)
-            bn_scale(first, 4, gamma1_sb[0])
-            aggregate1(1, 0)
-            aggregate1(1, 1)
-            bn_bias(first, 4, beta1_sb[0])
-            aggregate1(1, 2)
-            aggregate1(1, 3)
-            bn_root(second, 4)
-            normalise_relu1(0)
-            bn_mean_gamma(second, 4, gamma1_sb[1])
-            bn_reciprocal(second, 4)
-            bn_mean_scale(second, 4)
-            bn_scale(second, 4, gamma1_sb[1])
-            bn_bias(second, 4, beta1_sb[1])
-            normalise_relu1(1)
-            maximum_over_points(0, 0)
-            maximum_over_points(0, 1)
-            maximum_over_points(1, 0)
-            maximum_over_points(1, 1)
-            store(0, nc.vector.tensor_copy)
-            store(1, nc.scalar.copy)
+        def channels_to_partitions(h):
+            for pair in range(2):
+                yT[h, pair] = work.tile([P, 2, ROWS], F32, name="yT_ps", tag="work")
+                for c in range(2):
+                    for m in range(POINTS):
+                        nc.tensor.transpose(yT[h, pair][:, c, m * VOXELS : (m + 1) * VOXELS], y_sb[h][:, m, (2 * pair + c) * P : (2 * pair + c + 1) * P], ident_f32[:])
+            stats1[h] = tail.tile([P, 4, 6], F32, name="stats1")
+            mean_var["y1", h] = tail.tile([P, 4, 2], F32, name="mean_var1")
+
+        def statistics1(h, c):
+            nc.vector.bn_stats(out=stats1[h][:, c, :], in_=yT[h, c // 2][:, c % 2, :])
+
+        def aggregate1(h, c):
+            nc.vector.bn_aggr(out=mean_var["y1", h][:, c, :], in_=stats1[h][:, c, :])
+
+        def normalise_relu1(h):
+            z[h] = tail.tile([P, 4, POINTS, VOXELS], F32, name="z")
+            for c in range(4):
+                nc.scalar.activation(out=z[h][:, c].rearrange("p m v -> p (m v)"), in_=yT[h, c // 2][:, c % 2, :], func=ACT.Relu, bias=bn[("y1", h), "b"][:, c : c + 1], scale=bn[("y1", h), "s"][:, c : c + 1])
+            z_max[h] = tail.tile([P, 4, VOXELS], F32, name="z_max")
+            o_ps[h] = work.tile([P, 4, P], F32, name="o_ps", tag="work")
+
+        def maximum_over_points(h, pair):
+            chunks = slice(2 * pair, 2 * pair + 2)
+            nc.vector.tensor_tensor(out=z_max[h][:, chunks, :], in0=z[h][:, chunks, 0, :], in1=z[h][:, chunks, 1, :], op=ALU.max)
+            for c in range(2 * pair, 2 * pair + 2):
+                nc.tensor.transpose(o_ps[h][:, c, :], z_max[h][:, c, :], ident_f32[:])
+
+        def store(h, copy):
+            o_sb = tail.tile([P, N_HALF], F32, name="o_sb")
+            copy(out=o_sb[:], in_=o_ps[h][:].rearrange("v c n -> v (c n)"))
+            nc.sync.dma_start(out=out[:, h * N_HALF : (h + 1) * N_HALF], in_=o_sb[:])
+
+        gamma1_sb = [gb1[:, 0, 4 * h : 4 * h + 4] for h in range(HALVES)]
+        beta1_sb = [gb1[:, 1, 4 * h : 4 * h + 4] for h in range(HALVES)]
+        first, second = ("y1", 0), ("y1", 1)
+        leave_psum(0)
+        leave_psum(1)
+        channels_to_partitions(0)
+        channels_to_partitions(1)
+        statistics1(0, 0)
+        statistics1(0, 1)
+        statistics1(0, 2)
+        aggregate1(0, 0)
+        statistics1(0, 3)
+        aggregate1(0, 1)
+        aggregate1(0, 2)
+        statistics1(1, 0)
+        aggregate1(0, 3)
+        bn_root(first, 4)
+        statistics1(1, 1)
+        bn_mean_gamma(first, 4, gamma1_sb[0])
+        statistics1(1, 2)
+        bn_reciprocal(first, 4)
+        statistics1(1, 3)
+        bn_mean_scale(first, 4)
+        bn_scale(first, 4, gamma1_sb[0])
+        aggregate1(1, 0)
+        aggregate1(1, 1)
+        bn_bias(first, 4, beta1_sb[0])
+        aggregate1(1, 2)
+        aggregate1(1, 3)
+        bn_root(second, 4)
+        normalise_relu1(0)
+        bn_mean_gamma(second, 4, gamma1_sb[1])
+        bn_reciprocal(second, 4)
+        bn_mean_scale(second, 4)
+        bn_scale(second, 4, gamma1_sb[1])
+        bn_bias(second, 4, beta1_sb[1])
+        normalise_relu1(1)
+        maximum_over_points(0, 0)
+        maximum_over_points(0, 1)
+        maximum_over_points(1, 0)
+        maximum_over_points(1, 1)
+        store(0, nc.vector.tensor_copy)
+        store(1, nc.scalar.copy)

@@ -51,10 +51,10 @@ def tile_vfe_k_kernel(tc, voxel_feats, W0, gamma0, beta0, W1_words, W1_scales, g
         ident_f32 = keep.tile([P, P], F32, name="ident_f32")
         warm = keep.tile([P, 2], F32, name="warm")
 
+        nc.vector.memset(w_planes[:].bitcast(I32), 0)
+        nc.vector.memset(params[:], 0.0)
         nc.vector.memset(warm[:], 1.0)
         nc.scalar.activation(out=warm[:, 1:2], in_=warm[:, 0:1], func=ACT.Sqrt)
-        nc.vector.memset(params[:], 0.0)
-        nc.vector.memset(w_planes[:].bitcast(I32), 0)
         make_identity(nc, ident_bf[:])
         make_identity(nc, ident_f32[:])
 
@@ -198,23 +198,29 @@ def tile_vfe_k_kernel(tc, voxel_feats, W0, gamma0, beta0, W1_words, W1_scales, g
             nc.sync.dma_start(out=vf_sb[:], in_=voxel_feats)
             w0_view = W0.rearrange("(g p t) c -> p g (t c)", p=P, t=PACK)
             w0_sb = [w0_rows.tile([P, 2 * PACK, C_IN], BF16, name="w0_sb%d" % pair) for pair in range(GROUPS // 2)]
+
+            def load_scale_rows(n):
+                batch, rest = divmod(n, 2 * 4)
+                half, Q = divmod(rest, 4)
+                i = batch + half * (GROUPS // PLANES)
+                nc.sync.dma_start(
+                    out=w_planes[32 * Q : 32 * Q + 16, i, :].bitcast(I32),
+                    in_=W1_scales[PLANES * i : PLANES * (i + 1), 4 * Q : 4 * Q + 4, :].bitcast(I32),
+                )
+
             for pair in range(GROUPS // 2):
                 nc.sync.dma_start(out=w0_sb[pair][:].rearrange("p (g t) c -> p g (t c)", g=2), in_=w0_view[:, 2 * pair : 2 * pair + 2, :])
+                load_scale_rows(pair)
                 if pair == 0:
                     nc.sync.dma_start(out=params[0:GROUPS, 0:K_PASS], in_=gamma0.rearrange("(g k) -> g k", k=K_PASS))
                     nc.sync.dma_start(out=params[GROUPS : 2 * GROUPS, 0:K_PASS], in_=beta0.rearrange("(g k) -> g k", k=K_PASS))
                     nc.sync.dma_start(out=params[0:CHUNKS, K_PASS:], in_=gamma1.rearrange("(j i) -> j i", i=P))
                     nc.sync.dma_start(out=params[CHUNKS : 2 * CHUNKS, K_PASS:], in_=beta1.rearrange("(j i) -> j i", i=P))
-            for batch in range(GROUPS // PLANES):
-                for i in (batch, GROUPS // PLANES + batch):
-                    for Q in range(4):
-                        nc.sync.dma_start(
-                            out=w_planes[32 * Q : 32 * Q + 16, i, :].bitcast(I32),
-                            in_=W1_scales[PLANES * i : PLANES * (i + 1), 4 * Q : 4 * Q + 4, :].bitcast(I32),
-                        )
-                for g in range(PLANES * batch, PLANES * (batch + 1)):
-                    for G in (g, GROUPS + g):
-                        nc.sync.dma_start(out=w_words[G][:].bitcast(I32), in_=W1_words[G].rearrange("p n t -> p (n t)").bitcast(I32))
+            for g in range(GROUPS):
+                for part, G in enumerate((g, GROUPS + g)):
+                    nc.sync.dma_start(out=w_words[G][:].bitcast(I32), in_=W1_words[G].rearrange("p n t -> p (n t)").bitcast(I32))
+                    if g < GROUPS - PLANES:
+                        load_scale_rows(GROUPS // 2 + 2 * g + part)
 
             def turn_w0(pair):
                 wT_ps = turn.tile([P, 2 * PACK, P], BF16, name="wT_ps")

from contextlib import ExitStack

import concourse.mybir as mybir
from concourse.masks import make_identity

F32 = mybir.dt.float32
BF16 = mybir.dt.bfloat16
I32 = mybir.dt.int32
U32 = mybir.dt.uint32
U8 = mybir.dt.uint8
FP8X4 = mybir.dt.float8_e4m3fn_x4
ACT = mybir.ActivationFunctionType
ALU = mybir.AluOpType

P = 128
PACK = 4
K_PASS = P * PACK
VOXELS = 128
POINTS = 2
ROWS = VOXELS * POINTS
C_IN = 128
C0 = 8192
C1 = 1024
GROUPS = C0 // K_PASS
N_HALF = 512
HALVES = C1 // N_HALF
CHUNKS = C1 // P
EPS = 1e-3
PLANES = 4

FLOPS = 2 * ROWS * C_IN * C0 + 2 * ROWS * 2 * C0 * C1


def tile_vfe_k_kernel(tc, voxel_feats, W0, gamma0, beta0, W1_words, W1_scales, gamma1, beta1, out):
    nc = tc.nc
    with ExitStack() as ctx:
        ctx.enter_context(tc.manual_schedule())
        keep = ctx.enter_context(tc.tile_pool(name="keep", bufs=1))
        ring = ctx.enter_context(tc.tile_pool(name="ring", bufs=3))
        work = ctx.enter_context(tc.psum_pool(name="work", bufs=4))

        vf_sb = keep.tile([P, POINTS, C_IN], BF16, name="vf_sb")
        vfT = keep.tile([P, ROWS], BF16, name="vfT")
        params = keep.tile([P, K_PASS + P], BF16, name="params")
        gb0 = keep.tile([P, 2, GROUPS, PACK], F32, name="gb0")
        gb1 = keep.tile([P, 2, CHUNKS], F32, name="gb1")
        w0T = [keep.tile([P, 2 * PACK, P], BF16, name="w0T%d" % pair) for pair in range(GROUPS // 2)]
        w_words = [keep.tile([P, C1 * PACK], U8, name="w_words%d" % G, align_bytes=64) for G in range(2 * GROUPS)]
        w_planes = keep.tile([P, 2 * GROUPS // PLANES, C1], U8, name="w_planes", align_bytes=64)
        ident_bf = keep.tile([P, P], BF16, name="ident_bf")
        ident_f32 = keep.tile([P, P], F32, name="ident_f32")
        warm = keep.tile([P, 2], F32, name="warm")

        nc.vector.memset(w_planes[:].bitcast(I32), 0)
        nc.vector.memset(params[:], 0.0)
        nc.vector.memset(warm[:], 1.0)
        nc.scalar.activation(out=warm[:, 1:2], in_=warm[:, 0:1], func=ACT.Sqrt)
        make_identity(nc, ident_bf[:])
        make_identity(nc, ident_f32[:])

        def weight_operands(G, h):
            k = PLANES * (G % PLANES)
            words = w_words[G][:, h * N_HALF * PACK : (h + 1) * N_HALF * PACK].bitcast(FP8X4)
            return words, w_planes[k:P, G // PLANES, h * N_HALF : (h + 1) * N_HALF]

        mean_var = {}
        bn = {}

        def bn_tile(key, name, width):
            bn[key, name] = ring.tile([P, width], F32, name=name + str(width))
            return bn[key, name]

        def bn_root(key, width):
            nc.scalar.activation(out=bn_tile(key, "std", width)[:], in_=mean_var[key][:, :, 1], func=ACT.Sqrt, bias=EPS, scale=1.0)

        def bn_mean_gamma(key, width, gamma):
            nc.vector.tensor_tensor(out=bn_tile(key, "mg", width)[:], in0=mean_var[key][:, :, 0], in1=gamma, op=ALU.mult)

        def bn_reciprocal(key, width):
            nc.vector.reciprocal(out=bn_tile(key, "rstd", width)[:], in_=bn[key, "std"][:])

        def bn_mean_scale(key, width):
            nc.vector.tensor_tensor(out=bn_tile(key, "ms", width)[:], in0=bn[key, "mg"][:], in1=bn[key, "rstd"][:], op=ALU.mult)

        def bn_scale(key, width, gamma):
            nc.vector.tensor_tensor(out=bn_tile(key, "s", width)[:], in0=gamma, in1=bn[key, "rstd"][:], op=ALU.mult)

        def bn_bias(key, width, beta):
            nc.vector.tensor_tensor(out=bn_tile(key, "b", width)[:], in0=beta, in1=bn[key, "ms"][:], op=ALU.subtract)

        y0 = {}
        stats = {}
        planes = {}
        grouped = {}
        a_grouped = {}
        x_codes = {}
        x_scales = {}

        def is_group(g):
            return 0 <= g < GROUPS

        def layer0_matmuls(g):
            for u in range(2):
                y0[g, u] = work.tile([P, 2, ROWS], F32, name="y0_ps", tag="work")
                for e in range(2):
                    nc.tensor.matmul(y0[g, u][:, e, :], lhsT=w0T[g // 2][:, (g % 2) * PACK + 2 * u + e, :], rhs=vfT[:], start=True, stop=True)
            stats[g] = ring.tile([P, PACK, 6], F32, name="stats")
            mean_var[g] = ring.tile([P, PACK, 2], F32, name="mean_var")

        def statistics(g, t):
            nc.vector.bn_stats(out=stats[g][:, t, :], in_=y0[g, t // 2][:, t % 2, :])

        def aggregate(g, t):
            nc.vector.bn_aggr(out=mean_var[g][:, t, :], in_=stats[g][:, t, :])

        def normalise_relu(g):
            planes[g] = ring.tile([P, PACK, ROWS], BF16, name="planes")
            for t in range(PACK):
                nc.scalar.activation(out=planes[g][:, t, :], in_=y0[g, t // 2][:, t % 2, :], func=ACT.Relu, bias=bn[g, "b"][:, t : t + 1], scale=bn[g, "s"][:, t : t + 1])

        def regroup(g):
            grouped[g] = ring.tile([P, POINTS, VOXELS, PACK], BF16, name="grouped", align_bytes=64)
            for m in range(POINTS):
                nc.scalar.copy(
                    out=grouped[g][:, m].rearrange("p (c i) t -> p c t i", i=4),
                    in_=planes[g][:, :, m * VOXELS : (m + 1) * VOXELS].rearrange("p t (c i) -> p c t i", i=4),
                )

        def maximum(g):
            a_grouped[g] = ring.tile([P, VOXELS, PACK], BF16, name="a_grouped", align_bytes=64)
            nc.vector.tensor_tensor(out=a_grouped[g][:], in0=grouped[g][:, 0], in1=grouped[g][:, 1], op=ALU.max)

        def quantise_p(g):
            x_codes[g] = ring.tile([P, POINTS + 1, VOXELS], U32, name="x_codes", align_bytes=64)
            x_scales[g] = ring.tile([P, POINTS + 1, VOXELS], U8, name="x_scales", align_bytes=64)
            nc.vector.quantize_mx(
                out=x_codes[g][:, 0:POINTS, :].rearrange("p m v -> p (m v)").bitcast(FP8X4),
                scales=x_scales[g][:, 0:POINTS, :].rearrange("p m v -> p (m v)"),
                in_=grouped[g][:].rearrange("p m v t -> p (m v t)"),
            )

        def quantise_a(g):
            nc.vector.quantize_mx(out=x_codes[g][:, POINTS, :].bitcast(FP8X4), scales=x_scales[g][:, POINTS, :], in_=a_grouped[g][:].rearrange("p v t -> p (v t)"))

        def mx_passes(g):
            for h in range(HALVES):
                for m in range(POINTS):
                    for operand, G in ((m, g), (POINTS, GROUPS + g)):
                        words, plane = weight_operands(G, h)
                        nc.tensor.matmul_mx(
                            acc[m][h][:],
                            lhsT=x_codes[g][:, operand, :].bitcast(FP8X4),
                            lhsT_scale=x_scales[g][:, operand, :],
                            rhs=words,
                            rhs_scale=plane,
                            start=(G == 0),
                            stop=(G == 2 * GROUPS - 1),
                        )

        def step(i):
            done, soon, new = i - 1, i + 1, i + 2
            if is_group(i):
                normalise_relu(i)
            if is_group(soon):
                bn_root(soon, PACK)
            if is_group(i):
                regroup(i)
            if is_group(new):
                layer0_matmuls(new)
            if is_group(done):
                maximum(done)
            if is_group(soon):
                bn_mean_gamma(soon, PACK, gb0[:, 0, soon, :])
            if is_group(done):
                quantise_p(done)
                quantise_a(done)
                mx_passes(done)
            if is_group(soon):
                bn_reciprocal(soon, PACK)
            if is_group(new):
                statistics(new, 0)
            if is_group(soon):
                bn_mean_scale(soon, PACK)
                bn_scale(soon, PACK, gb0[:, 0, soon, :])
            if is_group(new):
                statistics(new, 1)
            if is_group(soon):
                bn_bias(soon, PACK, gb0[:, 1, soon, :])
            if is_group(new):
                statistics(new, 2)
                aggregate(new, 0)
                statistics(new, 3)
                aggregate(new, 1)
                aggregate(new, 2)
                aggregate(new, 3)

        with tc.tile_pool(name="w0_rows", bufs=1) as w0_rows, tc.psum_pool(name="turn", bufs=4) as turn:
            nc.sync.dma_start(out=vf_sb[:], in_=voxel_feats)
            w0_view = W0.rearrange("(g p t) c -> p g (t c)", p=P, t=PACK)
            w0_sb = [w0_rows.tile([P, 2 * PACK, C_IN], BF16, name="w0_sb%d" % pair) for pair in range(GROUPS // 2)]

            def load_scale_rows(n):
                batch, rest = divmod(n, 2 * 4)
                half, Q = divmod(rest, 4)
                i = batch + half * (GROUPS // PLANES)
                nc.sync.dma_start(
                    out=w_planes[32 * Q : 32 * Q + 16, i, :].bitcast(I32),
                    in_=W1_scales[PLANES * i : PLANES * (i + 1), 4 * Q : 4 * Q + 4, :].bitcast(I32),
                )

            for pair in range(GROUPS // 2):
                nc.sync.dma_start(out=w0_sb[pair][:].rearrange("p (g t) c -> p g (t c)", g=2), in_=w0_view[:, 2 * pair : 2 * pair + 2, :])
                load_scale_rows(pair)
                if pair == 0:
                    nc.sync.dma_start(out=params[0:GROUPS, 0:K_PASS], in_=gamma0.rearrange("(g k) -> g k", k=K_PASS))
                    nc.sync.dma_start(out=params[GROUPS : 2 * GROUPS, 0:K_PASS], in_=beta0.rearrange("(g k) -> g k", k=K_PASS))
                    nc.sync.dma_start(out=params[0:CHUNKS, K_PASS:], in_=gamma1.rearrange("(j i) -> j i", i=P))
                    nc.sync.dma_start(out=params[CHUNKS : 2 * CHUNKS, K_PASS:], in_=beta1.rearrange("(j i) -> j i", i=P))
            for g in range(GROUPS):
                for part, G in enumerate((g, GROUPS + g)):
                    nc.sync.dma_start(out=w_words[G][:].bitcast(I32), in_=W1_words[G].rearrange("p n t -> p (n t)").bitcast(I32))
                    if g < GROUPS - PLANES:
                        load_scale_rows(GROUPS // 2 + 2 * g + part)

            def turn_w0(pair):
                wT_ps = turn.tile([P, 2 * PACK, P], BF16, name="wT_ps")
                for j in range(2 * PACK):
                    nc.tensor.transpose(wT_ps[:, j, :], w0_sb[pair][:, j, :], ident_bf[:])
                if pair % 2 == 0:
                    nc.vector.tensor_copy(out=w0T[pair][:], in_=wT_ps[:])
                else:
                    nc.scalar.copy(out=w0T[pair][:], in_=wT_ps[:])

            vT_ps = turn.tile([P, POINTS, VOXELS], BF16, name="vT_ps", tag="wT_ps")
            for m in range(POINTS):
                nc.tensor.transpose(vT_ps[:, m, :], vf_sb[:, m, :], ident_bf[:])
            nc.vector.tensor_copy(out=vfT[:], in_=vT_ps[:].rearrange("c m v -> c (m v)"))
            turn_w0(0)

            step(-2)
            pT_ps = turn.tile([P, PACK + 1, P], BF16, name="pT_ps", tag="wT_ps")
            for t in range(PACK):
                nc.tensor.transpose(pT_ps[:, t, :], params[:, t:K_PASS:PACK], ident_bf[:])
            nc.tensor.transpose(pT_ps[:, PACK, :], params[:, K_PASS:], ident_bf[:])
            nc.vector.tensor_copy(out=gb0[:], in_=pT_ps[:, 0:PACK, 0 : 2 * GROUPS].rearrange("p t (w g) -> p w g t", w=2))
            nc.vector.tensor_copy(out=gb1[:], in_=pT_ps[:, PACK, 0 : 2 * CHUNKS].rearrange("p (w j) -> p w j", w=2))
            for pair in range(1, GROUPS // 4):
                turn_w0(pair)
            step(-1)
            for pair in range(GROUPS // 4, GROUPS // 2):
                turn_w0(pair)

        tail = ctx.enter_context(tc.tile_pool(name="tail", bufs=2))
        acc_pool = ctx.enter_context(tc.psum_pool(name="acc", bufs=1))
        acc = [[acc_pool.tile([P, N_HALF], F32, name="acc%d%d" % (m, h)) for h in range(HALVES)] for m in range(POINTS)]

        for i in range(GROUPS + 1):
            step(i)

        y_sb = {}
        yT = {}
        stats1 = {}
        z = {}
        z_max = {}
        o_ps = {}

        def leave_psum(h):
            y_sb[h] = tail.tile([P, POINTS, N_HALF], F32, name="y_sb")
            nc.scalar.copy(out=y_sb[h][:, 0, :], in_=acc[0][h][:])
            nc.vector.tensor_copy(out=y_sb[h][:, 1, :], in_=acc[1][h][:])

        def channels_to_partitions(h):
            for pair in range(2):
                yT[h, pair] = work.tile([P, 2, ROWS], F32, name="yT_ps", tag="work")
                for c in range(2):
                    for m in range(POINTS):
                        nc.tensor.transpose(yT[h, pair][:, c, m * VOXELS : (m + 1) * VOXELS], y_sb[h][:, m, (2 * pair + c) * P : (2 * pair + c + 1) * P], ident_f32[:])
            stats1[h] = tail.tile([P, 4, 6], F32, name="stats1")
            mean_var["y1", h] = tail.tile([P, 4, 2], F32, name="mean_var1")

        def statistics1(h, c):
            nc.vector.bn_stats(out=stats1[h][:, c, :], in_=yT[h, c // 2][:, c % 2, :])

        def aggregate1(h, c):
            nc.vector.bn_aggr(out=mean_var["y1", h][:, c, :], in_=stats1[h][:, c, :])

        def normalise_relu1(h):
            z[h] = tail.tile([P, 4, POINTS, VOXELS], F32, name="z")
            for c in range(4):
                nc.scalar.activation(out=z[h][:, c].rearrange("p m v -> p (m v)"), in_=yT[h, c // 2][:, c % 2, :], func=ACT.Relu, bias=bn[("y1", h), "b"][:, c : c + 1], scale=bn[("y1", h), "s"][:, c : c + 1])
            z_max[h] = tail.tile([P, 4, VOXELS], F32, name="z_max")
            o_ps[h] = work.tile([P, 4, P], F32, name="o_ps", tag="work")

        def maximum_over_points(h, pair):
            chunks = slice(2 * pair, 2 * pair + 2)
            nc.vector.tensor_tensor(out=z_max[h][:, chunks, :], in0=z[h][:, chunks, 0, :], in1=z[h][:, chunks, 1, :], op=ALU.max)
            for c in range(2 * pair, 2 * pair + 2):
                nc.tensor.transpose(o_ps[h][:, c, :], z_max[h][:, c, :], ident_f32[:])

        def store(h, copy):
            o_sb = tail.tile([P, N_HALF], F32, name="o_sb")
            copy(out=o_sb[:], in_=o_ps[h][:].rearrange("v c n -> v (c n)"))
            nc.sync.dma_start(out=out[:, h * N_HALF : (h + 1) * N_HALF], in_=o_sb[:])

        gamma1_sb = [gb1[:, 0, 4 * h : 4 * h + 4] for h in range(HALVES)]
        beta1_sb = [gb1[:, 1, 4 * h : 4 * h + 4] for h in range(HALVES)]
        first, second = ("y1", 0), ("y1", 1)
        leave_psum(0)
        leave_psum(1)
        channels_to_partitions(0)
        channels_to_partitions(1)
        statistics1(0, 0)
        statistics1(0, 1)
        statistics1(0, 2)
        aggregate1(0, 0)
        statistics1(0, 3)
        aggregate1(0, 1)
        aggregate1(0, 2)
        statistics1(1, 0)
        aggregate1(0, 3)
        bn_root(first, 4)
        statistics1(1, 1)
        bn_mean_gamma(first, 4, gamma1_sb[0])
        statistics1(1, 2)
        bn_reciprocal(first, 4)
        statistics1(1, 3)
        bn_mean_scale(first, 4)
        bn_scale(first, 4, gamma1_sb[0])
        aggregate1(1, 0)
        aggregate1(1, 1)
        bn_bias(first, 4, beta1_sb[0])
        aggregate1(1, 2)
        aggregate1(1, 3)
        bn_root(second, 4)
        normalise_relu1(0)
        bn_mean_gamma(second, 4, gamma1_sb[1])
        bn_reciprocal(second, 4)
        bn_mean_scale(second, 4)
        bn_scale(second, 4, gamma1_sb[1])
        bn_bias(second, 4, beta1_sb[1])
        normalise_relu1(1)
        maximum_over_points(0, 0)
        maximum_over_points(0, 1)
        maximum_over_points(1, 0)
        maximum_over_points(1, 1)
        store(0, nc.vector.tensor_copy)
        store(1, nc.scalar.copy)
